import numpy as np
import ml_dtypes


def mxq(x, axis, fmt="e4m3"):
    dtype, down = {"e4m3": (ml_dtypes.float8_e4m3fn, 7), "e5m2": (ml_dtypes.float8_e5m2, 14)}[fmt]
    v = np.moveaxis(np.asarray(x, np.float32).astype(ml_dtypes.bfloat16).astype(np.float64), axis, -1)
    blocks = v.reshape(v.shape[:-1] + (-1, 32))
    amax = np.abs(blocks).max(-1, keepdims=True)
    byte = np.maximum(np.where(amax > 0, np.frexp(amax)[1] - 1 + 127, 0) - down, 1)
    scale = np.exp2(byte - 127.0)
    codes = (blocks / scale).astype(np.float32).astype(dtype).astype(np.float64)
    return np.moveaxis((codes * scale).reshape(v.shape), -1, axis)


WIDE = False


def mx_kscale(k):
    if not WIDE:
        return np.ones(k)
    levels = np.array([10, -10, 5, -5, 0])
    if k % 512:
        return np.exp2(np.random.permutation(np.resize(levels, k // 32))).repeat(32)
    a = np.empty((k // 512, 16))
    for p in range(k // 512):
        a[p, :8] = np.random.permutation(np.resize(levels, 8))
        for g in range(8):
            far = levels[np.abs(levels - a[p, g]) >= 10]
            a[p, g + 8] = far[np.random.randint(len(far))]
    return np.exp2(a.ravel()).repeat(32)


BF16 = ml_dtypes.bfloat16


def bf(x):
    return np.asarray(x, np.float32).astype(BF16)


def f64(x):
    return np.asarray(x).astype(np.float64)


SIZE, DIM, FDIM = 3072, 512, 2048
EPS = 1e-5


def setup_inputs():
    s = mx_kscale(DIM)
    r = np.random.uniform(0.4, 2.0, (SIZE, 1))
    g = np.random.standard_normal((SIZE, DIM))
    return {"lt_weight": bf(g * s / np.sqrt(np.sum(s * s)) * r),
            "Lambdas": bf(np.random.standard_normal((DIM, FDIM)) * 1.5 * np.sqrt(np.mean(s * s)) / s[:, None]),
            "bias": bf(np.random.uniform(0.0, 2.0 * np.pi, FDIM))}


def reference(lt_weight, Lambdas, bias):
    x = f64(lt_weight)
    norms = np.linalg.norm(x, axis=-1, keepdims=True)
    maxnorm = 1.0 - EPS
    e_all = x * np.minimum(1.0, maxnorm / np.maximum(norms, EPS))
    scale = np.sqrt(2.0) / np.sqrt(DIM)
    return scale * np.cos((mxq(e_all, 1, "e4m3") @ mxq(f64(Lambdas), 0, "e4m3")) + f64(bias))

@@ -1,0 +1,308 @@
+import math
+from contextlib import ExitStack
+
+import concourse.mybir as mybir
+from concourse.masks import make_identity
+
+F32 = mybir.dt.float32
+BF16 = mybir.dt.bfloat16
+I32 = mybir.dt.int32
+U32 = mybir.dt.uint32
+U8 = mybir.dt.uint8
+FP8X4 = mybir.dt.float8_e4m3fn_x4
+ALU = mybir.AluOpType
+ACT = mybir.ActivationFunctionType
+
+SIZE, DIM, FDIM = 3072, 512, 2048
+EPS = 1e-5
+TWO_PI = 2.0 * math.pi
+FACTOR = math.sqrt(2.0 / DIM)
+FLOPS = 2 * SIZE * DIM * FDIM
+
+P = 128
+PACK = 4
+NB = 512
+NT = SIZE // P
+NCHUNK = SIZE // NB
+NFB = FDIM // P
+NQUARTER = FDIM // NB
+NBANK = NCHUNK * NFB
+NPAIR = NBANK // 2
+PAIRS_PER_CHUNK = NFB // 2
+
+LEAVE, WHOLE, FRACTION, TURN, SINE, FINISH = 1, 2, 3, 4, 5, 6
+AHEAD = 4
+
+
+def tensor_subtracts(q):
+    return q % 2 == 1
+
+
+def tile_rff_kernel(tc, lt_weight, Lambdas, bias, out):
+    nc = tc.nc
+    x_view = lt_weight.rearrange("(p n) k -> p n k", n=NT)
+    out_view = out.rearrange("(p n) f -> p n f", n=NT)
+    lam_view = Lambdas.rearrange("(p t) f -> p t f", t=PACK)
+
+    with ExitStack() as ctx:
+        keep = ctx.enter_context(tc.tile_pool(name="keep", bufs=1))
+        stage = ctx.enter_context(tc.tile_pool(name="stage", bufs=2))
+        bank = ctx.enter_context(tc.tile_pool(name="bank", bufs=6))
+        ints = ctx.enter_context(tc.tile_pool(name="ints", bufs=3))
+        nega = ctx.enter_context(tc.tile_pool(name="nega", bufs=3))
+        work = ctx.enter_context(tc.tile_pool(name="work", bufs=4))
+        psum_m = ctx.enter_context(tc.psum_pool(name="psum_m", bufs=4))
+        psum_t = ctx.enter_context(tc.psum_pool(name="psum_t", bufs=4))
+        ctx.enter_context(tc.manual_schedule())
+
+        x_sb = keep.tile([P, NT, DIM], BF16)
+        e_sb = keep.tile([P, NT, DIM], BF16)
+        lam_raw = keep.tile([P, PACK, FDIM], BF16)
+        lam_g = keep.tile([P, FDIM, PACK], BF16, align_bytes=64)
+        lam_codes = keep.tile([P, FDIM], U32, align_bytes=64)
+        lam_scales = keep.tile([P, FDIM], U8, align_bytes=64)
+        e_codes = keep.tile([P, SIZE], U32, align_bytes=64)
+        e_scales = keep.tile([P, SIZE], U8, align_bytes=64)
+        bias_rows = keep.tile([P, P], BF16)
+        phase = keep.tile([P, NFB], F32)
+        ident = keep.tile([P, P], BF16)
+        ident_f = keep.tile([P, P], F32)
+        warm = keep.tile([P, 1], F32)
+        n2 = keep.tile([P, NT], F32)
+        nrm = keep.tile([P, NT], F32)
+        floor = keep.tile([P, NT], F32)
+        rcp = keep.tile([P, NT], F32)
+        fac = keep.tile([P, NT], F32)
+
+
+        def load_x(c):
+            nc.sync.dma_start(out=x_sb[:, 4 * c:4 * c + 4, :], in_=x_view[:, 4 * c:4 * c + 4, :])
+
+        def load_lam(v):
+            cols = slice(v * NB, (v + 1) * NB)
+            nc.sync.dma_start(out=lam_raw[:, :, cols], in_=lam_view[:, :, cols])
+
+        def squares(c):
+            for n in range(4 * c, 4 * c + 4):
+                junk = stage.tile([P, DIM], BF16)
+                nc.scalar.activation(out=junk[:], in_=x_sb[:, n, :], func=ACT.Square, accum_out=n2[:, n:n + 1])
+
+        def root(first, last):
+            nc.scalar.activation(out=nrm[:, first:last], in_=n2[:, first:last], func=ACT.Sqrt)
+
+        def clip_factor(first, last, link):
+            tiles = slice(first, last)
+            if link == 0:
+                nc.vector.tensor_scalar_max(out=floor[:, tiles], in0=nrm[:, tiles], scalar1=EPS)
+            elif link == 1:
+                nc.vector.reciprocal(out=rcp[:, tiles], in_=floor[:, tiles])
+            else:
+                nc.vector.tensor_scalar(out=fac[:, tiles], in0=rcp[:, tiles], scalar1=1.0 - EPS, scalar2=1.0,
+                                        op0=ALU.mult, op1=ALU.min)
+
+        def clip(n):
+            nc.vector.tensor_scalar(out=e_sb[:, n, :], in0=x_sb[:, n, :], scalar1=fac[:, n:n + 1], scalar2=None,
+                                    op0=ALU.mult)
+
+        flipped = {}
+        grouped = {}
+
+        def flip(c, h):
+            flipped[c, h] = psum_m.tile([P, 2, 2, P], F32, name="flipped", tag="acc")
+            for d in range(2):
+                words = e_sb[:, 4 * c + 2 * h + d, :].bitcast(F32)
+                for u in range(2):
+                    nc.tensor.transpose(flipped[c, h][:, d, u, :], words[:, u::2], ident_f[:])
+
+        def gather(c, h):
+            if h == 0:
+                grouped[c] = stage.tile([P, 4 * P * PACK], BF16, name="grouped", align_bytes=64)
+            half = grouped[c][:, 2 * h * P * PACK:2 * (h + 1) * P * PACK].bitcast(F32)
+            nc.vector.tensor_copy(out=half.rearrange("p (d r u) -> p d r u", d=2, u=2),
+                                  in_=flipped[c, h][:].rearrange("p d u r -> p d r u"))
+
+        def quantise_e(c):
+            cols = slice(c * NB, (c + 1) * NB)
+            nc.vector.quantize_mx(out=e_codes[:, cols].bitcast(FP8X4), scales=e_scales[:, cols],
+                                  in_=grouped[c][:])
+
+        def regroup_lam(v):
+            cols = slice(v * NB, (v + 1) * NB)
+            nc.vector.tensor_copy(out=lam_g[:, cols, :].rearrange("p (y w) t -> p y t w", w=4),
+                                  in_=lam_raw[:, :, cols].rearrange("p t (y w) -> p y t w", w=4))
+
+        def quantise_lam(v):
+            cols = slice(v * NB, (v + 1) * NB)
+            nc.vector.quantize_mx(out=lam_codes[:, cols].bitcast(FP8X4), scales=lam_scales[:, cols],
+                                  in_=lam_g[:, cols, :].rearrange("p f t -> p (f t)"))
+
+
+        acc = {}
+        turns = {}
+        whole = {}
+        minus = {}
+        back = {}
+        res = {}
+
+        def product(j):
+            c, fb = divmod(j, NFB)
+            feats = slice(fb * P, (fb + 1) * P)
+            rows = slice(c * NB, (c + 1) * NB)
+            acc[j] = psum_m.tile([P, NB], F32, name="acc")
+            nc.tensor.matmul_mx(out=acc[j][:], lhsT=lam_codes[:, feats].bitcast(FP8X4), lhsT_scale=lam_scales[:, feats],
+                                rhs=e_codes[:, rows].bitcast(FP8X4), rhs_scale=e_scales[:, rows], start=True, stop=True)
+
+        def leave(j):
+            q, odd = divmod(j, 2)
+            fb = j % NFB
+            if odd == 0:
+                turns[q] = bank.tile([P, 2, NB], F32, name="turns")
+            nc.scalar.activation(out=turns[q][:, odd, :], in_=acc[j][:], func=ACT.Identity, scale=1.0 / TWO_PI,
+                                 bias=phase[:, fb:fb + 1])
+
+        def whole_turns(q):
+            whole[q] = ints.tile([P, 2, NB], I32, name="whole")
+            if tensor_subtracts(q):
+                nc.vector.tensor_scalar(out=whole[q][:], in0=turns[q][:], scalar1=-1.0, scalar2=None, op0=ALU.mult)
+            else:
+                nc.vector.tensor_copy(out=whole[q][:], in_=turns[q][:])
+
+        def fraction(q):
+            if tensor_subtracts(q):
+                minus[q] = nega.tile([P, 2, NB], F32, name="minus")
+                nc.vector.tensor_copy(out=minus[q][:], in_=whole[q][:])
+            else:
+                nc.vector.tensor_tensor(out=turns[q][:], in0=turns[q][:], in1=whole[q][:], op=ALU.subtract)
+
+        def turn_back(j):
+            q, odd = divmod(j, 2)
+            back[j] = psum_t.tile([P, NB], F32, name="back")
+            for a in range(4):
+                blk = slice(a * P, (a + 1) * P)
+                if tensor_subtracts(q):
+                    nc.tensor.matmul(out=back[j][:, blk], lhsT=turns[q][:, odd, blk], rhs=ident_f[:], is_transpose=True,
+                                     start=True, stop=False)
+                    nc.tensor.matmul(out=back[j][:, blk], lhsT=minus[q][:, odd, blk], rhs=ident_f[:], is_transpose=True,
+                                     start=False, stop=True)
+                else:
+                    nc.tensor.transpose(back[j][:, blk], turns[q][:, odd, blk], ident_f[:])
+
+        def sine(j):
+            u, b = divmod(j, 4)
+            if b == 0:
+                res[u] = work.tile([P, 4, NB], F32, name="res")
+            nc.scalar.activation(out=res[u][:, :, b * P:(b + 1) * P], in_=back[j][:].rearrange("p (a f) -> p a f", a=4),
+                                 func=ACT.Sin, scale=TWO_PI)
+
+        def finish(q):
+            u, side = divmod(q, 2)
+            c, v = divmod(u, NQUARTER)
+            left = side * 2 * P
+            piece = res[u][:, :, left:left + 2 * P]
+            nc.vector.tensor_scalar(out=piece, in0=piece, scalar1=FACTOR, scalar2=None, op0=ALU.mult)
+            nc.sync.dma_start(out=out_view[:, 4 * c:4 * c + 4, v * NB + left:v * NB + left + 2 * P], in_=piece)
+
+        def banks(q):
+            return [j for j in (2 * q, 2 * q + 1) if 0 <= q < NPAIR]
+
+        def pairs(q):
+            return [q] if 0 <= q < NPAIR else []
+
+
+        nc.vector.memset(bias_rows[:], 0.0)
+        nc.vector.memset(warm[:], 1.0)
+        load_x(0)
+        nc.sync.dma_start(out=bias_rows[0:NFB, :], in_=bias.rearrange("(fb f) -> fb f", f=P))
+        load_lam(0)
+        load_x(1)
+        load_lam(1)
+        load_x(2)
+        load_lam(2)
+        load_lam(3)
+        load_x(3)
+        load_x(4)
+        load_x(5)
+
+        nc.scalar.activation(out=warm[:], in_=warm[:], func=ACT.Sqrt)
+        make_identity(nc, ident[:])
+        make_identity(nc, ident_f[:])
+
+        squares(0)
+        root(0, 4)
+        squares(1)
+        root(4, 8)
+        for c in range(2, NCHUNK):
+            squares(c)
+        root(8, NT)
+
+        bias_t = psum_t.tile([P, P], BF16, name="bias_t", tag="back")
+        nc.tensor.transpose(bias_t[:], bias_rows[:], ident[:])
+        nc.vector.tensor_scalar(out=phase[:], in0=bias_t[:, 0:NFB], scalar1=0.5 * math.pi, scalar2=1.0 / TWO_PI,
+                                op0=ALU.add, op1=ALU.mult)
+
+        regroup_lam(0)
+        for link in range(3):
+            clip_factor(0, 4, link)
+        for n in range(0, 4):
+            clip(n)
+        flip(0, 0)
+        flip(0, 1)
+        regroup_lam(1)
+        gather(0, 0)
+        regroup_lam(2)
+        gather(0, 1)
+        quantise_lam(0)
+        clip_factor(4, 8, 0)
+        regroup_lam(3)
+        clip_factor(4, 8, 1)
+        quantise_e(0)
+        clip_factor(4, 8, 2)
+        quantise_lam(1)
+        for n in range(4, 8):
+            clip(n)
+        flip(1, 0)
+        flip(1, 1)
+        quantise_lam(2)
+        quantise_lam(3)
+        gather(1, 0)
+        gather(1, 1)
+        for j in banks(0):
+            product(j)
+        clip_factor(8, NT, 0)
+        quantise_e(1)
+        clip_factor(8, NT, 1)
+
+
+        for s in range(NPAIR + FINISH + 1):
+            c_front, part = divmod(s + AHEAD, PAIRS_PER_CHUNK)
+            c_front += 1
+            if not 2 <= c_front < NCHUNK:
+                part = -1
+
+            for j in banks(s - LEAVE):
+                leave(j)
+            if s > 0:
+                for j in banks(s):
+                    product(j)
+            for j in banks(s - TURN):
+                turn_back(j)
+            if part in (2, 4):
+                flip(c_front, part // 2 - 1)
+            for j in banks(s - SINE):
+                sine(j)
+
+            for q in pairs(s - WHOLE):
+                whole_turns(q)
+            if s == 1:
+                clip_factor(8, NT, 2)
+            if part in (0, 1):
+                clip(4 * c_front + 2 * part)
+                clip(4 * c_front + 2 * part + 1)
+            if part in (3, 5):
+                gather(c_front, part // 2 - 1)
+            if part == 7:
+                quantise_e(c_front)
+            for q in pairs(s - FRACTION):
+                fraction(q)
+            for q in pairs(s - FINISH):
+                finish(q)

@@ -25,17 +25,21 @@ NB = 512
 NT = SIZE // P
 NCHUNK = SIZE // NB
 NFB = FDIM // P
-NQUARTER = FDIM // NB
+NPIECE = 8
+PW = FDIM // NPIECE
 NBANK = NCHUNK * NFB
 NPAIR = NBANK // 2
 PAIRS_PER_CHUNK = NFB // 2
 
 LEAVE, WHOLE, FRACTION, TURN, SINE, FINISH = 1, 2, 3, 4, 5, 6
-AHEAD = 4
 
 
 def tensor_subtracts(q):
-    return q % 2 == 1
+    return True
+
+
+def vector_leaves(j):
+    return j >= NBANK - 4 or (j >= NFB and j % 4 == 1 and (j < 2 * NFB or j % 8 == 1))
 
 
 def tile_rff_kernel(tc, lt_weight, Lambdas, bias, out):
@@ -57,7 +61,7 @@ def tile_rff_kernel(tc, lt_weight, Lambdas, bias, out):
 
         x_sb = keep.tile([P, NT, DIM], BF16)
         e_sb = keep.tile([P, NT, DIM], BF16)
-        lam_raw = keep.tile([P, PACK, FDIM], BF16)
+        lam_raw = [keep.tile([P, PACK, PW], BF16, name=f"lam_raw{v}") for v in range(NPIECE)]
         lam_g = keep.tile([P, FDIM, PACK], BF16, align_bytes=64)
         lam_codes = keep.tile([P, FDIM], U32, align_bytes=64)
         lam_scales = keep.tile([P, FDIM], U8, align_bytes=64)
@@ -69,36 +73,33 @@ def tile_rff_kernel(tc, lt_weight, Lambdas, bias, out):
         ident_f = keep.tile([P, P], F32)
         warm = keep.tile([P, 1], F32)
         n2 = keep.tile([P, NT], F32)
-        nrm = keep.tile([P, NT], F32)
         floor = keep.tile([P, NT], F32)
         rcp = keep.tile([P, NT], F32)
         fac = keep.tile([P, NT], F32)
+        minus_half = keep.tile([P, NT], F32)
 
 
-        def load_x(c):
-            nc.sync.dma_start(out=x_sb[:, 4 * c:4 * c + 4, :], in_=x_view[:, 4 * c:4 * c + 4, :])
+        def load_x(first, last):
+            nc.sync.dma_start(out=x_sb[:, first:last, :], in_=x_view[:, first:last, :])
 
         def load_lam(v):
-            cols = slice(v * NB, (v + 1) * NB)
-            nc.sync.dma_start(out=lam_raw[:, :, cols], in_=lam_view[:, :, cols])
+            nc.sync.dma_start(out=lam_raw[v][:], in_=lam_view[:, :, v * PW:(v + 1) * PW])
 
-        def squares(c):
-            for n in range(4 * c, 4 * c + 4):
-                junk = stage.tile([P, DIM], BF16)
-                nc.scalar.activation(out=junk[:], in_=x_sb[:, n, :], func=ACT.Square, accum_out=n2[:, n:n + 1])
+        def squares_s(n):
+            junk = stage.tile([P, DIM], BF16, name="junk_s")
+            nc.scalar.activation(out=junk[:], in_=x_sb[:, n, :], func=ACT.Square, accum_out=n2[:, n:n + 1])
 
-        def root(first, last):
-            nc.scalar.activation(out=nrm[:, first:last], in_=n2[:, first:last], func=ACT.Sqrt)
+        def squares_v(n):
+            junk = stage.tile([P, DIM], BF16, name="junk_v")
+            nc.vector.scalar_tensor_tensor(out=junk[:], in0=x_sb[:, n, :], scalar=1.0, in1=x_sb[:, n, :],
+                                           op0=ALU.mult, op1=ALU.mult, accum_out=n2[:, n:n + 1])
 
-        def clip_factor(first, last, link):
-            tiles = slice(first, last)
-            if link == 0:
-                nc.vector.tensor_scalar_max(out=floor[:, tiles], in0=nrm[:, tiles], scalar1=EPS)
-            elif link == 1:
-                nc.vector.reciprocal(out=rcp[:, tiles], in_=floor[:, tiles])
-            else:
-                nc.vector.tensor_scalar(out=fac[:, tiles], in0=rcp[:, tiles], scalar1=1.0 - EPS, scalar2=1.0,
-                                        op0=ALU.mult, op1=ALU.min)
+        def clip_factor(c):
+            tiles = slice(4 * c, 4 * c + 4)
+            nc.gpsimd.tensor_scalar(out=floor[:, tiles], in0=n2[:, tiles], scalar1=EPS * EPS, scalar2=None, op0=ALU.max)
+            nc.gpsimd.tensor_tensor(out=rcp[:, tiles], in0=floor[:, tiles], in1=minus_half[:, tiles], op=ALU.pow)
+            nc.gpsimd.tensor_scalar(out=fac[:, tiles], in0=rcp[:, tiles], scalar1=1.0 - EPS, scalar2=1.0,
+                                    op0=ALU.mult, op1=ALU.min)
 
         def clip(n):
             nc.vector.tensor_scalar(out=e_sb[:, n, :], in0=x_sb[:, n, :], scalar1=fac[:, n:n + 1], scalar2=None,
@@ -114,25 +115,22 @@ def tile_rff_kernel(tc, lt_weight, Lambdas, bias, out):
                 for u in range(2):
                     nc.tensor.transpose(flipped[c, h][:, d, u, :], words[:, u::2], ident_f[:])
 
-        def gather(c, h):
+        def gather(c, h, copy):
             if h == 0:
                 grouped[c] = stage.tile([P, 4 * P * PACK], BF16, name="grouped", align_bytes=64)
             half = grouped[c][:, 2 * h * P * PACK:2 * (h + 1) * P * PACK].bitcast(F32)
-            nc.vector.tensor_copy(out=half.rearrange("p (d r u) -> p d r u", d=2, u=2),
-                                  in_=flipped[c, h][:].rearrange("p d u r -> p d r u"))
+            copy(out=half.rearrange("p (d r u) -> p d r u", d=2, u=2), in_=flipped[c, h][:].rearrange("p d u r -> p d r u"))
 
         def quantise_e(c):
             cols = slice(c * NB, (c + 1) * NB)
-            nc.vector.quantize_mx(out=e_codes[:, cols].bitcast(FP8X4), scales=e_scales[:, cols],
-                                  in_=grouped[c][:])
+            nc.vector.quantize_mx(out=e_codes[:, cols].bitcast(FP8X4), scales=e_scales[:, cols], in_=grouped[c][:])
 
         def regroup_lam(v):
-            cols = slice(v * NB, (v + 1) * NB)
-            nc.vector.tensor_copy(out=lam_g[:, cols, :].rearrange("p (y w) t -> p y t w", w=4),
-                                  in_=lam_raw[:, :, cols].rearrange("p t (y w) -> p y t w", w=4))
+            nc.vector.tensor_copy(out=lam_g[:, v * PW:(v + 1) * PW, :].rearrange("p (y w) t -> p y t w", w=4),
+                                  in_=lam_raw[v][:].rearrange("p t (y w) -> p y t w", w=4))
 
         def quantise_lam(v):
-            cols = slice(v * NB, (v + 1) * NB)
+            cols = slice(v * PW, (v + 1) * PW)
             nc.vector.quantize_mx(out=lam_codes[:, cols].bitcast(FP8X4), scales=lam_scales[:, cols],
                                   in_=lam_g[:, cols, :].rearrange("p f t -> p (f t)"))
 
@@ -157,8 +155,12 @@ def tile_rff_kernel(tc, lt_weight, Lambdas, bias, out):
             fb = j % NFB
             if odd == 0:
                 turns[q] = bank.tile([P, 2, NB], F32, name="turns")
-            nc.scalar.activation(out=turns[q][:, odd, :], in_=acc[j][:], func=ACT.Identity, scale=1.0 / TWO_PI,
-                                 bias=phase[:, fb:fb + 1])
+            if vector_leaves(j):
+                nc.vector.tensor_scalar(out=turns[q][:, odd, :], in0=acc[j][:], scalar1=1.0 / TWO_PI,
+                                        scalar2=phase[:, fb:fb + 1], op0=ALU.mult, op1=ALU.add)
+            else:
+                nc.scalar.activation(out=turns[q][:, odd, :], in_=acc[j][:], func=ACT.Identity, scale=1.0 / TWO_PI,
+                                     bias=phase[:, fb:fb + 1])
 
         def whole_turns(q):
             whole[q] = ints.tile([P, 2, NB], I32, name="whole")
@@ -194,13 +196,13 @@ def tile_rff_kernel(tc, lt_weight, Lambdas, bias, out):
             nc.scalar.activation(out=res[u][:, :, b * P:(b + 1) * P], in_=back[j][:].rearrange("p (a f) -> p a f", a=4),
                                  func=ACT.Sin, scale=TWO_PI)
 
-        def finish(q):
-            u, side = divmod(q, 2)
-            c, v = divmod(u, NQUARTER)
-            left = side * 2 * P
-            piece = res[u][:, :, left:left + 2 * P]
+        def finish(j, count):
+            u, b = divmod(j, 4)
+            c, v = divmod(u, FDIM // NB)
+            piece = res[u][:, :, b * P:(b + count) * P]
             nc.vector.tensor_scalar(out=piece, in0=piece, scalar1=FACTOR, scalar2=None, op0=ALU.mult)
-            nc.sync.dma_start(out=out_view[:, 4 * c:4 * c + 4, v * NB + left:v * NB + left + 2 * P], in_=piece)
+            left = v * NB + b * P
+            nc.sync.dma_start(out=out_view[:, 4 * c:4 * c + 4, left:left + count * P], in_=piece)
 
         def banks(q):
             return [j for j in (2 * q, 2 * q + 1) if 0 <= q < NPAIR]
@@ -211,98 +213,89 @@ def tile_rff_kernel(tc, lt_weight, Lambdas, bias, out):
 
         nc.vector.memset(bias_rows[:], 0.0)
         nc.vector.memset(warm[:], 1.0)
-        load_x(0)
-        nc.sync.dma_start(out=bias_rows[0:NFB, :], in_=bias.rearrange("(fb f) -> fb f", f=P))
+        nc.gpsimd.memset(minus_half[:], -0.5)
+        load_x(0, 2)
+        load_x(2, 4)
         load_lam(0)
-        load_x(1)
+        nc.sync.dma_start(out=bias_rows[0:NFB, :], in_=bias.rearrange("(fb f) -> fb f", f=P))
+        load_x(4, 8)
         load_lam(1)
-        load_x(2)
         load_lam(2)
-        load_lam(3)
-        load_x(3)
-        load_x(4)
-        load_x(5)
+        load_x(8, 12)
+        for v in range(3, NPIECE):
+            load_lam(v)
+        for c in range(3, NCHUNK):
+            load_x(4 * c, 4 * c + 4)
 
-        nc.scalar.activation(out=warm[:], in_=warm[:], func=ACT.Sqrt)
-        make_identity(nc, ident[:])
+        nc.scalar.activation(out=warm[:], in_=warm[:], func=ACT.Sin)
         make_identity(nc, ident_f[:])
+        make_identity(nc, ident[:])
 
-        squares(0)
-        root(0, 4)
-        squares(1)
-        root(4, 8)
-        for c in range(2, NCHUNK):
-            squares(c)
-        root(8, NT)
-
-        bias_t = psum_t.tile([P, P], BF16, name="bias_t", tag="back")
-        nc.tensor.transpose(bias_t[:], bias_rows[:], ident[:])
-        nc.vector.tensor_scalar(out=phase[:], in0=bias_t[:, 0:NFB], scalar1=0.5 * math.pi, scalar2=1.0 / TWO_PI,
-                                op0=ALU.add, op1=ALU.mult)
-
+        squares_s(0)
+        squares_v(1)
+        squares_s(2)
+        squares_v(3)
+        clip_factor(0)
         regroup_lam(0)
-        for link in range(3):
-            clip_factor(0, 4, link)
         for n in range(0, 4):
             clip(n)
+        quantise_lam(0)
         flip(0, 0)
         flip(0, 1)
-        regroup_lam(1)
-        gather(0, 0)
-        regroup_lam(2)
-        gather(0, 1)
-        quantise_lam(0)
-        clip_factor(4, 8, 0)
-        regroup_lam(3)
-        clip_factor(4, 8, 1)
-        quantise_e(0)
-        clip_factor(4, 8, 2)
-        quantise_lam(1)
+        bias_t = psum_t.tile([P, P], BF16, name="bias_t", tag="back")
+        nc.tensor.transpose(bias_t[:], bias_rows[:], ident[:])
         for n in range(4, 8):
-            clip(n)
-        flip(1, 0)
-        flip(1, 1)
-        quantise_lam(2)
-        quantise_lam(3)
-        gather(1, 0)
-        gather(1, 1)
-        for j in banks(0):
-            product(j)
-        clip_factor(8, NT, 0)
-        quantise_e(1)
-        clip_factor(8, NT, 1)
+            squares_s(n)
+        clip_factor(1)
+        gather(0, 0, nc.vector.tensor_copy)
+        gather(0, 1, nc.scalar.copy)
+        nc.vector.tensor_scalar(out=phase[:], in0=bias_t[:, 0:NFB], scalar1=0.5 * math.pi, scalar2=1.0 / TWO_PI,
+                                op0=ALU.add, op1=ALU.mult)
+        quantise_e(0)
+        regroup_lam(1)
+        regroup_lam(2)
+        quantise_lam(1)
 
 
         for s in range(NPAIR + FINISH + 1):
-            c_front, part = divmod(s + AHEAD, PAIRS_PER_CHUNK)
+            c_front, part = divmod(s, PAIRS_PER_CHUNK)
             c_front += 1
-            if not 2 <= c_front < NCHUNK:
+            if c_front >= NCHUNK:
                 part = -1
 
+            for j in banks(s):
+                product(j)
             for j in banks(s - LEAVE):
                 leave(j)
-            if s > 0:
-                for j in banks(s):
-                    product(j)
             for j in banks(s - TURN):
                 turn_back(j)
             if part in (2, 4):
                 flip(c_front, part // 2 - 1)
+            if 8 + s < NT:
+                squares_s(8 + s)
+                if s % 4 == 3:
+                    clip_factor(2 + s // 4)
             for j in banks(s - SINE):
                 sine(j)
 
             for q in pairs(s - WHOLE):
                 whole_turns(q)
-            if s == 1:
-                clip_factor(8, NT, 2)
+            if s + 3 < NPIECE:
+                regroup_lam(s + 3)
             if part in (0, 1):
                 clip(4 * c_front + 2 * part)
                 clip(4 * c_front + 2 * part + 1)
             if part in (3, 5):
-                gather(c_front, part // 2 - 1)
-            if part == 7:
+                gather(c_front, part // 2 - 1, nc.vector.tensor_copy)
+            if part == 6:
                 quantise_e(c_front)
             for q in pairs(s - FRACTION):
                 fraction(q)
+            if s + 2 < NPIECE:
+                quantise_lam(s + 2)
             for q in pairs(s - FINISH):
-                finish(q)
+                if q < NPAIR - 1:
+                    finish(2 * q, 2)
+                else:
+                    finish(2 * q, 1)
+                    finish(2 * q + 1, 1)

@@ -35,11 +35,11 @@ LEAVE, WHOLE, FRACTION, TURN, SINE, FINISH = 1, 2, 3, 4, 5, 6
 
 
 def tensor_subtracts(q):
-    return True
+    return q % 2 == 1
 
 
 def vector_leaves(j):
-    return j >= NBANK - 4 or (j >= NFB and j % 4 == 1 and (j < 2 * NFB or j % 8 == 1))
+    return j >= NBANK - 4 or (NFB <= j < 2 * NFB and j % 4 == 1)
 
 
 def tile_rff_kernel(tc, lt_weight, Lambdas, bias, out):

@@ -35,11 +35,11 @@ LEAVE, WHOLE, FRACTION, TURN, SINE, FINISH = 1, 2, 3, 4, 5, 6
 
 
 def tensor_subtracts(q):
-    return q % 2 == 1
+    return q < 8 or q % 4 != 0
 
 
 def vector_leaves(j):
-    return j >= NBANK - 4 or (NFB <= j < 2 * NFB and j % 4 == 1)
+    return j >= NBANK - 4 and j % 2 == 1 or (j >= NFB and j % 4 == 1 and j < 64) or (j >= 64 and j % 8 == 1)
 
 
 def tile_rff_kernel(tc, lt_weight, Lambdas, bias, out):
@@ -99,6 +99,13 @@ def tile_rff_kernel(tc, lt_weight, Lambdas, bias, out):
             nc.gpsimd.tensor_scalar(out=floor[:, tiles], in0=n2[:, tiles], scalar1=EPS * EPS, scalar2=None, op0=ALU.max)
             nc.gpsimd.tensor_tensor(out=rcp[:, tiles], in0=floor[:, tiles], in1=minus_half[:, tiles], op=ALU.pow)
             nc.gpsimd.tensor_scalar(out=fac[:, tiles], in0=rcp[:, tiles], scalar1=1.0 - EPS, scalar2=1.0,
+                                    op0=ALU.mult, op1=ALU.min)
+
+        def root(first, last):
+            nc.scalar.activation(out=rcp[:, first:last], in_=n2[:, first:last], func=ACT.Abs_reciprocal_sqrt, bias=1e-30)
+
+        def clip_factor_v(first, last):
+            nc.vector.tensor_scalar(out=fac[:, first:last], in0=rcp[:, first:last], scalar1=1.0 - EPS, scalar2=1.0,
                                     op0=ALU.mult, op1=ALU.min)
 
         def clip(n):
@@ -227,41 +234,47 @@ def tile_rff_kernel(tc, lt_weight, Lambdas, bias, out):
         for c in range(3, NCHUNK):
             load_x(4 * c, 4 * c + 4)
 
-        nc.scalar.activation(out=warm[:], in_=warm[:], func=ACT.Sin)
+        nc.scalar.activation(out=warm[:], in_=warm[:], func=ACT.Abs_reciprocal_sqrt)
         make_identity(nc, ident_f[:])
         make_identity(nc, ident[:])
 
         squares_s(0)
         squares_v(1)
-        squares_s(2)
+        root(0, 2)
         squares_v(3)
-        clip_factor(0)
-        regroup_lam(0)
-        for n in range(0, 4):
-            clip(n)
-        quantise_lam(0)
+        clip_factor_v(0, 2)
+        clip(0)
+        clip(1)
         flip(0, 0)
+        squares_s(2)
+        root(2, 4)
+        clip_factor_v(2, 4)
+        clip(2)
+        clip(3)
         flip(0, 1)
+        regroup_lam(0)
         bias_t = psum_t.tile([P, P], BF16, name="bias_t", tag="back")
         nc.tensor.transpose(bias_t[:], bias_rows[:], ident[:])
-        for n in range(4, 8):
-            squares_s(n)
-        clip_factor(1)
+        squares_s(4)
         gather(0, 0, nc.vector.tensor_copy)
         gather(0, 1, nc.scalar.copy)
+        for n in (5, 6, 7):
+            squares_s(n)
+        root(4, 8)
+        nc.scalar.activation(out=warm[:], in_=warm[:], func=ACT.Sin)
+        quantise_lam(0)
         nc.vector.tensor_scalar(out=phase[:], in0=bias_t[:, 0:NFB], scalar1=0.5 * math.pi, scalar2=1.0 / TWO_PI,
                                 op0=ALU.add, op1=ALU.mult)
         quantise_e(0)
         regroup_lam(1)
         regroup_lam(2)
         quantise_lam(1)
+        clip_factor_v(4, 8)
 
 
         for s in range(NPAIR + FINISH + 1):
-            c_front, part = divmod(s, PAIRS_PER_CHUNK)
-            c_front += 1
-            if c_front >= NCHUNK:
-                part = -1
+            c_front = 1 + s // PAIRS_PER_CHUNK
+            part = s - max(1, PAIRS_PER_CHUNK * (c_front - 1)) if c_front < NCHUNK else -1
 
             for j in banks(s):
                 product(j)
@@ -271,10 +284,10 @@ def tile_rff_kernel(tc, lt_weight, Lambdas, bias, out):
                 turn_back(j)
             if part in (2, 4):
                 flip(c_front, part // 2 - 1)
-            if 8 + s < NT:
-                squares_s(8 + s)
-                if s % 4 == 3:
-                    clip_factor(2 + s // 4)
+            if s % 2 == 1 and s // 2 < NT - 8:
+                squares_s(8 + s // 2)
+                if s % 8 == 7:
+                    clip_factor(2 + s // 8)
             for j in banks(s - SINE):
                 sine(j)
 

@@ -284,10 +284,11 @@ def tile_rff_kernel(tc, lt_weight, Lambdas, bias, out):
                 turn_back(j)
             if part in (2, 4):
                 flip(c_front, part // 2 - 1)
-            if s % 2 == 1 and s // 2 < NT - 8:
-                squares_s(8 + s // 2)
-                if s % 8 == 7:
-                    clip_factor(2 + s // 8)
+            n = 8 + s if s < 4 else 10 + s // 2
+            if n < NT and (s < 4 or s % 2 == 0):
+                squares_s(n)
+                if n % 4 == 3:
+                    clip_factor(n // 4)
             for j in banks(s - SINE):
                 sine(j)
 

@@ -35,11 +35,11 @@ LEAVE, WHOLE, FRACTION, TURN, SINE, FINISH = 1, 2, 3, 4, 5, 6
 
 
 def tensor_subtracts(q):
-    return q < 8 or q % 4 != 0
+    return q < 8 or q % 8 != 0
 
 
 def vector_leaves(j):
-    return j >= NBANK - 4 and j % 2 == 1 or (j >= NFB and j % 4 == 1 and j < 64) or (j >= 64 and j % 8 == 1)
+    return (NFB <= j < 64 and j % 8 == 1) or (64 <= j < 88 and j % 8 == 1)
 
 
 def tile_rff_kernel(tc, lt_weight, Lambdas, bias, out):

@@ -39,7 +39,7 @@ def tensor_subtracts(q):
 
 
 def vector_leaves(j):
-    return (NFB <= j < 64 and j % 8 == 1) or (64 <= j < 88 and j % 8 == 1)
+    return (NFB <= j < 2 * NFB and j % 4 == 1) or (2 * NFB <= j and j % 8 == 1)
 
 
 def tile_rff_kernel(tc, lt_weight, Lambdas, bias, out):

@@ -35,11 +35,11 @@ LEAVE, WHOLE, FRACTION, TURN, SINE, FINISH = 1, 2, 3, 4, 5, 6
 
 
 def tensor_subtracts(q):
-    return q < 8 or q % 8 != 0
+    return q < 8 or q % 4 != 0
 
 
 def vector_leaves(j):
-    return (NFB <= j < 2 * NFB and j % 4 == 1) or (2 * NFB <= j and j % 8 == 1)
+    return NFB <= j < 4 * NFB and j % 8 == 1
 
 
 def tile_rff_kernel(tc, lt_weight, Lambdas, bias, out):

@@ -39,7 +39,7 @@ def tensor_subtracts(q):
 
 
 def vector_leaves(j):
-    return NFB <= j < 4 * NFB and j % 8 == 1
+    return NFB <= j and j % 8 == 1
 
 
 def tile_rff_kernel(tc, lt_weight, Lambdas, bias, out):
@@ -255,14 +255,13 @@ def tile_rff_kernel(tc, lt_weight, Lambdas, bias, out):
         regroup_lam(0)
         bias_t = psum_t.tile([P, P], BF16, name="bias_t", tag="back")
         nc.tensor.transpose(bias_t[:], bias_rows[:], ident[:])
-        squares_s(4)
         gather(0, 0, nc.vector.tensor_copy)
-        gather(0, 1, nc.scalar.copy)
-        for n in (5, 6, 7):
+        for n in (4, 5, 6, 7):
             squares_s(n)
         root(4, 8)
         nc.scalar.activation(out=warm[:], in_=warm[:], func=ACT.Sin)
         quantise_lam(0)
+        gather(0, 1, nc.vector.tensor_copy)
         nc.vector.tensor_scalar(out=phase[:], in0=bias_t[:, 0:NFB], scalar1=0.5 * math.pi, scalar2=1.0 / TWO_PI,
                                 op0=ALU.add, op1=ALU.mult)
         quantise_e(0)

@@ -35,11 +35,11 @@ LEAVE, WHOLE, FRACTION, TURN, SINE, FINISH = 1, 2, 3, 4, 5, 6
 
 
 def tensor_subtracts(q):
-    return q < 8 or q % 4 != 0
+    return q < 8 or q % 5 != 0
 
 
 def vector_leaves(j):
-    return NFB <= j and j % 8 == 1
+    return NFB <= j < 5 * NFB and j % 8 == 1
 
 
 def tile_rff_kernel(tc, lt_weight, Lambdas, bias, out):

import math
from contextlib import ExitStack

import concourse.mybir as mybir
from concourse.masks import make_identity

F32 = mybir.dt.float32
BF16 = mybir.dt.bfloat16
I32 = mybir.dt.int32
U32 = mybir.dt.uint32
U8 = mybir.dt.uint8
FP8X4 = mybir.dt.float8_e4m3fn_x4
ALU = mybir.AluOpType
ACT = mybir.ActivationFunctionType

SIZE, DIM, FDIM = 3072, 512, 2048
EPS = 1e-5
TWO_PI = 2.0 * math.pi
FACTOR = math.sqrt(2.0 / DIM)
FLOPS = 2 * SIZE * DIM * FDIM

P = 128
PACK = 4
NB = 512
NT = SIZE // P
NCHUNK = SIZE // NB
NFB = FDIM // P
NPIECE = 8
PW = FDIM // NPIECE
NBANK = NCHUNK * NFB
NPAIR = NBANK // 2
PAIRS_PER_CHUNK = NFB // 2

LEAVE, WHOLE, FRACTION, TURN, SINE, FINISH = 1, 2, 3, 4, 5, 6


def tensor_subtracts(q):
    return q < 8 or q % 5 != 0


def vector_leaves(j):
    return NFB <= j < 5 * NFB and j % 8 == 1


def tile_rff_kernel(tc, lt_weight, Lambdas, bias, out):
    nc = tc.nc
    x_view = lt_weight.rearrange("(p n) k -> p n k", n=NT)
    out_view = out.rearrange("(p n) f -> p n f", n=NT)
    lam_view = Lambdas.rearrange("(p t) f -> p t f", t=PACK)

    with ExitStack() as ctx:
        keep = ctx.enter_context(tc.tile_pool(name="keep", bufs=1))
        stage = ctx.enter_context(tc.tile_pool(name="stage", bufs=2))
        bank = ctx.enter_context(tc.tile_pool(name="bank", bufs=6))
        ints = ctx.enter_context(tc.tile_pool(name="ints", bufs=3))
        nega = ctx.enter_context(tc.tile_pool(name="nega", bufs=3))
        work = ctx.enter_context(tc.tile_pool(name="work", bufs=4))
        psum_m = ctx.enter_context(tc.psum_pool(name="psum_m", bufs=4))
        psum_t = ctx.enter_context(tc.psum_pool(name="psum_t", bufs=4))
        ctx.enter_context(tc.manual_schedule())

        x_sb = keep.tile([P, NT, DIM], BF16)
        e_sb = keep.tile([P, NT, DIM], BF16)
        lam_raw = [keep.tile([P, PACK, PW], BF16, name=f"lam_raw{v}") for v in range(NPIECE)]
        lam_g = keep.tile([P, FDIM, PACK], BF16, align_bytes=64)
        lam_codes = keep.tile([P, FDIM], U32, align_bytes=64)
        lam_scales = keep.tile([P, FDIM], U8, align_bytes=64)
        e_codes = keep.tile([P, SIZE], U32, align_bytes=64)
        e_scales = keep.tile([P, SIZE], U8, align_bytes=64)
        bias_rows = keep.tile([P, P], BF16)
        phase = keep.tile([P, NFB], F32)
        ident = keep.tile([P, P], BF16)
        ident_f = keep.tile([P, P], F32)
        warm = keep.tile([P, 1], F32)
        n2 = keep.tile([P, NT], F32)
        floor = keep.tile([P, NT], F32)
        rcp = keep.tile([P, NT], F32)
        fac = keep.tile([P, NT], F32)
        minus_half = keep.tile([P, NT], F32)


        def load_x(first, last):
            nc.sync.dma_start(out=x_sb[:, first:last, :], in_=x_view[:, first:last, :])

        def load_lam(v):
            nc.sync.dma_start(out=lam_raw[v][:], in_=lam_view[:, :, v * PW:(v + 1) * PW])

        def squares_s(n):
            junk = stage.tile([P, DIM], BF16, name="junk_s")
            nc.scalar.activation(out=junk[:], in_=x_sb[:, n, :], func=ACT.Square, accum_out=n2[:, n:n + 1])

        def squares_v(n):
            junk = stage.tile([P, DIM], BF16, name="junk_v")
            nc.vector.scalar_tensor_tensor(out=junk[:], in0=x_sb[:, n, :], scalar=1.0, in1=x_sb[:, n, :],
                                           op0=ALU.mult, op1=ALU.mult, accum_out=n2[:, n:n + 1])

        def clip_factor(c):
            tiles = slice(4 * c, 4 * c + 4)
            nc.gpsimd.tensor_scalar(out=floor[:, tiles], in0=n2[:, tiles], scalar1=EPS * EPS, scalar2=None, op0=ALU.max)
            nc.gpsimd.tensor_tensor(out=rcp[:, tiles], in0=floor[:, tiles], in1=minus_half[:, tiles], op=ALU.pow)
            nc.gpsimd.tensor_scalar(out=fac[:, tiles], in0=rcp[:, tiles], scalar1=1.0 - EPS, scalar2=1.0,
                                    op0=ALU.mult, op1=ALU.min)

        def root(first, last):
            nc.scalar.activation(out=rcp[:, first:last], in_=n2[:, first:last], func=ACT.Abs_reciprocal_sqrt, bias=1e-30)

        def clip_factor_v(first, last):
            nc.vector.tensor_scalar(out=fac[:, first:last], in0=rcp[:, first:last], scalar1=1.0 - EPS, scalar2=1.0,
                                    op0=ALU.mult, op1=ALU.min)

        def clip(n):
            nc.vector.tensor_scalar(out=e_sb[:, n, :], in0=x_sb[:, n, :], scalar1=fac[:, n:n + 1], scalar2=None,
                                    op0=ALU.mult)

        flipped = {}
        grouped = {}

        def flip(c, h):
            flipped[c, h] = psum_m.tile([P, 2, 2, P], F32, name="flipped", tag="acc")
            for d in range(2):
                words = e_sb[:, 4 * c + 2 * h + d, :].bitcast(F32)
                for u in range(2):
                    nc.tensor.transpose(flipped[c, h][:, d, u, :], words[:, u::2], ident_f[:])

        def gather(c, h, copy):
            if h == 0:
                grouped[c] = stage.tile([P, 4 * P * PACK], BF16, name="grouped", align_bytes=64)
            half = grouped[c][:, 2 * h * P * PACK:2 * (h + 1) * P * PACK].bitcast(F32)
            copy(out=half.rearrange("p (d r u) -> p d r u", d=2, u=2), in_=flipped[c, h][:].rearrange("p d u r -> p d r u"))

        def quantise_e(c):
            cols = slice(c * NB, (c + 1) * NB)
            nc.vector.quantize_mx(out=e_codes[:, cols].bitcast(FP8X4), scales=e_scales[:, cols], in_=grouped[c][:])

        def regroup_lam(v):
            nc.vector.tensor_copy(out=lam_g[:, v * PW:(v + 1) * PW, :].rearrange("p (y w) t -> p y t w", w=4),
                                  in_=lam_raw[v][:].rearrange("p t (y w) -> p y t w", w=4))

        def quantise_lam(v):
            cols = slice(v * PW, (v + 1) * PW)
            nc.vector.quantize_mx(out=lam_codes[:, cols].bitcast(FP8X4), scales=lam_scales[:, cols],
                                  in_=lam_g[:, cols, :].rearrange("p f t -> p (f t)"))


        acc = {}
        turns = {}
        whole = {}
        minus = {}
        back = {}
        res = {}

        def product(j):
            c, fb = divmod(j, NFB)
            feats = slice(fb * P, (fb + 1) * P)
            rows = slice(c * NB, (c + 1) * NB)
            acc[j] = psum_m.tile([P, NB], F32, name="acc")
            nc.tensor.matmul_mx(out=acc[j][:], lhsT=lam_codes[:, feats].bitcast(FP8X4), lhsT_scale=lam_scales[:, feats],
                                rhs=e_codes[:, rows].bitcast(FP8X4), rhs_scale=e_scales[:, rows], start=True, stop=True)

        def leave(j):
            q, odd = divmod(j, 2)
            fb = j % NFB
            if odd == 0:
                turns[q] = bank.tile([P, 2, NB], F32, name="turns")
            if vector_leaves(j):
                nc.vector.tensor_scalar(out=turns[q][:, odd, :], in0=acc[j][:], scalar1=1.0 / TWO_PI,
                                        scalar2=phase[:, fb:fb + 1], op0=ALU.mult, op1=ALU.add)
            else:
                nc.scalar.activation(out=turns[q][:, odd, :], in_=acc[j][:], func=ACT.Identity, scale=1.0 / TWO_PI,
                                     bias=phase[:, fb:fb + 1])

        def whole_turns(q):
            whole[q] = ints.tile([P, 2, NB], I32, name="whole")
            if tensor_subtracts(q):
                nc.vector.tensor_scalar(out=whole[q][:], in0=turns[q][:], scalar1=-1.0, scalar2=None, op0=ALU.mult)
            else:
                nc.vector.tensor_copy(out=whole[q][:], in_=turns[q][:])

        def fraction(q):
            if tensor_subtracts(q):
                minus[q] = nega.tile([P, 2, NB], F32, name="minus")
                nc.vector.tensor_copy(out=minus[q][:], in_=whole[q][:])
            else:
                nc.vector.tensor_tensor(out=turns[q][:], in0=turns[q][:], in1=whole[q][:], op=ALU.subtract)

        def turn_back(j):
            q, odd = divmod(j, 2)
            back[j] = psum_t.tile([P, NB], F32, name="back")
            for a in range(4):
                blk = slice(a * P, (a + 1) * P)
                if tensor_subtracts(q):
                    nc.tensor.matmul(out=back[j][:, blk], lhsT=turns[q][:, odd, blk], rhs=ident_f[:], is_transpose=True,
                                     start=True, stop=False)
                    nc.tensor.matmul(out=back[j][:, blk], lhsT=minus[q][:, odd, blk], rhs=ident_f[:], is_transpose=True,
                                     start=False, stop=True)
                else:
                    nc.tensor.transpose(back[j][:, blk], turns[q][:, odd, blk], ident_f[:])

        def sine(j):
            u, b = divmod(j, 4)
            if b == 0:
                res[u] = work.tile([P, 4, NB], F32, name="res")
            nc.scalar.activation(out=res[u][:, :, b * P:(b + 1) * P], in_=back[j][:].rearrange("p (a f) -> p a f", a=4),
                                 func=ACT.Sin, scale=TWO_PI)

        def finish(j, count):
            u, b = divmod(j, 4)
            c, v = divmod(u, FDIM // NB)
            piece = res[u][:, :, b * P:(b + count) * P]
            nc.vector.tensor_scalar(out=piece, in0=piece, scalar1=FACTOR, scalar2=None, op0=ALU.mult)
            left = v * NB + b * P
            nc.sync.dma_start(out=out_view[:, 4 * c:4 * c + 4, left:left + count * P], in_=piece)

        def banks(q):
            return [j for j in (2 * q, 2 * q + 1) if 0 <= q < NPAIR]

        def pairs(q):
            return [q] if 0 <= q < NPAIR else []


        nc.vector.memset(bias_rows[:], 0.0)
        nc.vector.memset(warm[:], 1.0)
        nc.gpsimd.memset(minus_half[:], -0.5)
        load_x(0, 2)
        load_x(2, 4)
        load_lam(0)
        nc.sync.dma_start(out=bias_rows[0:NFB, :], in_=bias.rearrange("(fb f) -> fb f", f=P))
        load_x(4, 8)
        load_lam(1)
        load_lam(2)
        load_x(8, 12)
        for v in range(3, NPIECE):
            load_lam(v)
        for c in range(3, NCHUNK):
            load_x(4 * c, 4 * c + 4)

        nc.scalar.activation(out=warm[:], in_=warm[:], func=ACT.Abs_reciprocal_sqrt)
        make_identity(nc, ident_f[:])
        make_identity(nc, ident[:])

        squares_s(0)
        squares_v(1)
        root(0, 2)
        squares_v(3)
        clip_factor_v(0, 2)
        clip(0)
        clip(1)
        flip(0, 0)
        squares_s(2)
        root(2, 4)
        clip_factor_v(2, 4)
        clip(2)
        clip(3)
        flip(0, 1)
        regroup_lam(0)
        bias_t = psum_t.tile([P, P], BF16, name="bias_t", tag="back")
        nc.tensor.transpose(bias_t[:], bias_rows[:], ident[:])
        gather(0, 0, nc.vector.tensor_copy)
        for n in (4, 5, 6, 7):
            squares_s(n)
        root(4, 8)
        nc.scalar.activation(out=warm[:], in_=warm[:], func=ACT.Sin)
        quantise_lam(0)
        gather(0, 1, nc.vector.tensor_copy)
        nc.vector.tensor_scalar(out=phase[:], in0=bias_t[:, 0:NFB], scalar1=0.5 * math.pi, scalar2=1.0 / TWO_PI,
                                op0=ALU.add, op1=ALU.mult)
        quantise_e(0)
        regroup_lam(1)
        regroup_lam(2)
        quantise_lam(1)
        clip_factor_v(4, 8)


        for s in range(NPAIR + FINISH + 1):
            c_front = 1 + s // PAIRS_PER_CHUNK
            part = s - max(1, PAIRS_PER_CHUNK * (c_front - 1)) if c_front < NCHUNK else -1

            for j in banks(s):
                product(j)
            for j in banks(s - LEAVE):
                leave(j)
            for j in banks(s - TURN):
                turn_back(j)
            if part in (2, 4):
                flip(c_front, part // 2 - 1)
            n = 8 + s if s < 4 else 10 + s // 2
            if n < NT and (s < 4 or s % 2 == 0):
                squares_s(n)
                if n % 4 == 3:
                    clip_factor(n // 4)
            for j in banks(s - SINE):
                sine(j)

            for q in pairs(s - WHOLE):
                whole_turns(q)
            if s + 3 < NPIECE:
                regroup_lam(s + 3)
            if part in (0, 1):
                clip(4 * c_front + 2 * part)
                clip(4 * c_front + 2 * part + 1)
            if part in (3, 5):
                gather(c_front, part // 2 - 1, nc.vector.tensor_copy)
            if part == 6:
                quantise_e(c_front)
            for q in pairs(s - FRACTION):
                fraction(q)
            if s + 2 < NPIECE:
                quantise_lam(s + 2)
            for q in pairs(s - FINISH):
                if q < NPAIR - 1:
                    finish(2 * q, 2)
                else:
                    finish(2 * q, 1)
                    finish(2 * q + 1, 1)
